import numpy as np
import ml_dtypes


def mxq(x, axis, fmt="e4m3"):
    dtype, down = {"e4m3": (ml_dtypes.float8_e4m3fn, 7), "e5m2": (ml_dtypes.float8_e5m2, 14)}[fmt]
    v = np.moveaxis(np.asarray(x, np.float32).astype(ml_dtypes.bfloat16).astype(np.float64), axis, -1)
    blocks = v.reshape(v.shape[:-1] + (-1, 32))
    amax = np.abs(blocks).max(-1, keepdims=True)
    byte = np.maximum(np.where(amax > 0, np.frexp(amax)[1] - 1 + 127, 0) - down, 1)
    scale = np.exp2(byte - 127.0)
    codes = (blocks / scale).astype(np.float32).astype(dtype).astype(np.float64)
    return np.moveaxis((codes * scale).reshape(v.shape), -1, axis)


WIDE = False


def mx_kscale(k):
    if not WIDE:
        return np.ones(k)
    levels = np.array([10, -10, 5, -5, 0])
    if k % 512:
        return np.exp2(np.random.permutation(np.resize(levels, k // 32))).repeat(32)
    a = np.empty((k // 512, 16))
    for p in range(k // 512):
        a[p, :8] = np.random.permutation(np.resize(levels, 8))
        for g in range(8):
            far = levels[np.abs(levels - a[p, g]) >= 10]
            a[p, g + 8] = far[np.random.randint(len(far))]
    return np.exp2(a.ravel()).repeat(32)


BF16 = ml_dtypes.bfloat16


def bf(x):
    return np.asarray(x, np.float32).astype(BF16)


def f64(x):
    return np.asarray(x).astype(np.float64)


E2M1 = np.array([0.0, 0.5, 1.0, 1.5, 2.0, 3.0, 4.0, 6.0, -0.0, -0.5, -1.0, -1.5, -2.0, -3.0, -4.0, -6.0])


def pack_weight(w, fmt):
    k, n = w.shape
    w = f64(bf(w)).reshape(k // 32, 32, n)
    amax = np.abs(w).max(1)
    if fmt == "e4m3":
        byte = np.frexp(amax)[1] - 1 + 127 - 7
    else:
        mant, ex = np.frexp(amax / 6.0)
        byte = np.where(mant > 0.5, ex, ex - 1) + 127
    byte = np.clip(np.where(amax > 0, byte, 1), 1, 254)
    scaled = (w * np.exp2(127.0 - byte)[:, None, :]).reshape(k, n).astype(np.float32)
    by_word = np.ascontiguousarray(scaled.reshape(k // 512, 128, 4, n).transpose(0, 1, 3, 2))
    if fmt == "e4m3":
        words = by_word.astype(ml_dtypes.float8_e4m3fn).view(np.uint8)
    else:
        c = by_word.astype(ml_dtypes.float4_e2m1fn).view(np.uint8) & 0xF
        words = c[..., 0::2] | (c[..., 1::2] << 4)
    return np.ascontiguousarray(words), np.ascontiguousarray(byte.astype(np.uint8).reshape(k // 512, 16, n))


def unpack_weight(words, scales, fmt):
    g, p, n, _ = words.shape
    if fmt == "e4m3":
        vals = np.ascontiguousarray(words).view(ml_dtypes.float8_e4m3fn).astype(np.float64)
    else:
        nib = np.empty((g, p, n, 4), np.uint8)
        nib[..., 0::2] = words & 0xF
        nib[..., 1::2] = words >> 4
        vals = E2M1[nib]
    vals = vals * np.repeat(np.exp2(scales.astype(np.float64) - 127.0), 8, axis=1)[..., None]
    return vals.transpose(0, 1, 3, 2).reshape(g * 512, n)


B, T, C, N_HEAD, N_KV, D_LAT, D_ROPE = 2, 2048, 1024, 8, 4, 512, 64
HD = C // N_HEAD
D_NOPE = HD - D_ROPE
DR2 = D_ROPE // 2
ROPE_BASE = 10000.0
EPS = 1.1920928955078125e-07


def rope_tables():
    half = HD // 2
    inv_freq = 1.0 / (ROPE_BASE ** (np.arange(half) / half))
    ang = np.arange(T)[:, None] * inv_freq[None, :DR2]
    return np.cos(ang), np.sin(ang)


def rms(u):
    return u * (1.0 / np.sqrt(np.mean(u * u, axis=-1, keepdims=True) + EPS))


def draw0():
    s, t = mx_kscale(C), mx_kscale(D_LAT)
    cos, sin = rope_tables()
    x = bf(np.random.standard_normal((B, T, C)) * s)
    w_kv_words, w_kv_scales = pack_weight(np.random.standard_normal((C, D_LAT)) / np.sqrt(C) / s[:, None] * t, "e4m3")
    w_kup_words, w_kup_scales = pack_weight(np.random.standard_normal((D_LAT, N_KV * D_NOPE)) / np.sqrt(D_LAT) / t[:, None], "e4m3")
    w_vup_words, w_vup_scales = pack_weight(np.random.standard_normal((D_LAT, N_KV * HD)) / np.sqrt(D_LAT) / t[:, None], "e4m3")
    w_krope_words, w_krope_scales = pack_weight(np.random.standard_normal((C, N_KV * D_ROPE)) / np.sqrt(C) / s[:, None], "e4m3")
    return {"x": x,
            "cos": bf(cos), "sin": bf(sin),
            "w_kv_words": w_kv_words, "w_kv_scales": w_kv_scales,
            "w_kup_words": w_kup_words, "w_kup_scales": w_kup_scales,
            "w_vup_words": w_vup_words, "w_vup_scales": w_vup_scales,
            "w_krope_words": w_krope_words, "w_krope_scales": w_krope_scales}


def core(x, cos, sin, w_kv_words, w_kv_scales, w_kup_words, w_kup_scales, w_vup_words, w_vup_scales, w_krope_words, w_krope_scales):
    xq = mxq(f64(x), 2, "e4m3")
    latent = xq @ unpack_weight(w_kv_words, w_kv_scales, "e4m3")
    lq = mxq(latent, 2, "e4m3")
    k_nope = (lq @ unpack_weight(w_kup_words, w_kup_scales, "e4m3")).reshape(B, T, N_KV, D_NOPE)
    r = (xq @ unpack_weight(w_krope_words, w_krope_scales, "e4m3")).reshape(B, T, N_KV, D_ROPE)
    c, sn = f64(cos)[None, :, None, :], f64(sin)[None, :, None, :]
    r1, r2 = r[..., :DR2], r[..., DR2:]
    k_rope = np.concatenate([r1 * c + r2 * sn, -r1 * sn + r2 * c], axis=-1)
    k = rms(np.concatenate([k_rope, k_nope], axis=-1))
    v = (lq @ unpack_weight(w_vup_words, w_vup_scales, "e4m3")).reshape(B, T, N_KV, HD)
    return k, v


def e4m3fn_bytes(y):
    return np.clip(np.asarray(y, np.float64), -448.0, 448.0).astype(np.float32).astype(ml_dtypes.float8_e4m3fn).view(np.uint8)


def e4m3fn_values(b):
    return np.asarray(b, np.uint8).view(ml_dtypes.float8_e4m3fn).astype(np.float64)


def setup_inputs():
    d = draw0()
    x0 = np.asarray(d['x']).astype(np.float64)
    s = (np.max(np.abs(x0), axis=(0, 1), keepdims=True) / 448.0).astype(np.float32)
    out = {}
    for k, v in d.items():
        if k == 'x':
            out['x_bytes'] = e4m3fn_bytes(x0 / s.astype(np.float64))
            out['x_scale'] = s
        else:
            out[k] = v
    return out


def reference(x_bytes, x_scale, cos, sin, w_kv_words, w_kv_scales, w_kup_words, w_kup_scales, w_vup_words, w_vup_scales, w_krope_words, w_krope_scales):
    return core(e4m3fn_values(x_bytes) * x_scale.astype(np.float64), cos, sin, w_kv_words, w_kv_scales, w_kup_words, w_kup_scales, w_vup_words, w_vup_scales, w_krope_words, w_krope_scales)

@@ -1,0 +1,297 @@
+from contextlib import ExitStack
+
+import concourse.mybir as mybir
+from concourse.masks import make_identity
+
+B, T, C, DL = 2, 2048, 1024, 512
+NKV, HD, DR, DN = 4, 128, 64, 64
+TOK = B * T
+EPS = 1.1920928955078125e-07
+FLOPS = 2 * TOK * (C * DL + DL * NKV * DN + DL * NKV * HD + C * NKV * DR)
+
+F32 = mybir.dt.float32
+BF16 = mybir.dt.bfloat16
+I32 = mybir.dt.int32
+U32 = mybir.dt.uint32
+U8 = mybir.dt.uint8
+FP8 = mybir.dt.float8_e4m3fn
+FP8X4 = mybir.dt.float8_e4m3fn_x4
+ACT = mybir.ActivationFunctionType
+ALU = mybir.AluOpType
+
+P = 128
+RUN = 4
+NT = TOK // P
+NLOAD = NT // RUN
+
+
+def tile_mlacausalselfattention_pa_t_w8_kernel(
+    tc, x_bytes, x_scale, cos, sin, w_kv_words, w_kv_scales, w_kup_words, w_kup_scales,
+    w_vup_words, w_vup_scales, w_krope_words, w_krope_scales, out_k, out_v,
+):
+    nc = tc.nc
+    x_v = x_bytes.rearrange("b t k -> (b t) k").rearrange("(s p i) k -> s p i k", p=P, i=RUN)
+    k_v = out_k.rearrange("b t h d -> (b t) (h d)").rearrange("(s p i) c -> s i p c", p=P, i=RUN)
+    v_v = out_v.rearrange("b t h d -> (b t) (h d)").rearrange("(s p i) c -> s i p c", p=P, i=RUN)
+
+    with ExitStack() as ctx:
+        keep = ctx.enter_context(tc.tile_pool(name="keep", bufs=1))
+        xin = ctx.enter_context(tc.tile_pool(name="xin", bufs=NLOAD))
+        work = ctx.enter_context(tc.tile_pool(name="work", bufs=4))
+        small = ctx.enter_context(tc.tile_pool(name="small", bufs=5))
+        ps_x = ctx.enter_context(tc.psum_pool(name="ps_x", bufs=1))
+        ps_l = ctx.enter_context(tc.psum_pool(name="ps_l", bufs=3))
+        ps_k = ctx.enter_context(tc.psum_pool(name="ps_k", bufs=3))
+        ps_v = ctx.enter_context(tc.psum_pool(name="ps_v", bufs=1))
+        ctx.enter_context(tc.manual_schedule())
+
+        sc_raw = keep.tile([P, DL], U8, align_bytes=64, name="sc_raw")
+        sc_w = keep.tile([P, DL], U8, align_bytes=64, name="sc_w")
+        sc_kv = keep.tile([P, DL], U8, align_bytes=64, name="sc_kv")
+        dummy = keep.tile([P, 1], F32, name="dummy")
+        nc.vector.memset(dummy[:], 1.0)
+        nc.vector.memset(sc_raw[:].bitcast(I32), 0)
+        nc.vector.memset(sc_w[:].bitcast(I32), 0)
+        dummy_out = keep.tile([P, 1], F32, name="dummy_out")
+        nc.scalar.activation(dummy_out[:], dummy[:], ACT.Sqrt)
+        ident = keep.tile([P, P], F32, name="ident")
+        make_identity(nc, ident[:])
+
+        xs_scale = keep.tile([P, 2, 4], F32, name="xs_scale")
+        x_tiles = []
+        for s in range(NLOAD):
+            xt_in = xin.tile([P, RUN, C], U8, align_bytes=64, name="xt_in")
+            x_tiles.append(xt_in)
+        nc.sync.dma_start(out=x_tiles[0][:, 0, :], in_=x_v[0][:, 0, :])
+        nc.sync.dma_start(out=xs_scale[:], in_=x_scale.rearrange("a b (g p t) -> p (a b g) t", p=P, t=4))
+        nc.sync.dma_start(out=x_tiles[0][:, 1:RUN, :], in_=x_v[0][:, 1:RUN, :])
+        kv_raw = keep.tile([P, 2, DL], I32, align_bytes=64, name="kv_raw")
+        nc.sync.dma_start(out=kv_raw[:], in_=w_kv_words.rearrange("g p n t -> p g (n t)").bitcast(I32))
+        kv_s = w_kv_scales.bitcast(I32)
+        for q in range(4):
+            nc.sync.dma_start(out=sc_raw[32 * q : 32 * q + 8, :].bitcast(I32), in_=kv_s[:, 4 * q : 4 * q + 4, :])
+        kr_w = keep.tile([P, 2, NKV * DR], I32, align_bytes=64, name="kr_w")
+        nc.sync.dma_start(out=kr_w[:], in_=w_krope_words.rearrange("g p n t -> p g (n t)").bitcast(I32))
+        kr_s = w_krope_scales.bitcast(I32)
+        for q in range(4):
+            nc.sync.dma_start(
+                out=sc_w[32 * q + 8 : 32 * q + 16, 0 : NKV * DR].bitcast(I32), in_=kr_s[:, 4 * q : 4 * q + 4, :]
+            )
+        cs_in = keep.tile([P, 2, NT // 2, DR // 2], BF16, name="cs_in")
+        for j, src in enumerate((cos, sin)):
+            nc.sync.dma_start(
+                out=cs_in[:, j].rearrange("p (s i) c -> p s i c", i=RUN),
+                in_=src.rearrange("(s p i) c -> p s i c", p=P, i=RUN),
+            )
+        ku_w = keep.tile([P, NKV * DN], I32, align_bytes=64, name="ku_w")
+        nc.sync.dma_start(out=ku_w[:], in_=w_kup_words[0].rearrange("p n t -> p (n t)").bitcast(I32))
+        vu_w = keep.tile([P, NKV * HD], I32, align_bytes=64, name="vu_w")
+        nc.sync.dma_start(out=vu_w[:], in_=w_vup_words[0].rearrange("p n t -> p (n t)").bitcast(I32))
+        vu_s = w_vup_scales.bitcast(I32)
+        ku_s = w_kup_scales.bitcast(I32)
+        for q in range(4):
+            nc.sync.dma_start(out=sc_w[32 * q : 32 * q + 4, :].bitcast(I32), in_=vu_s[0, 4 * q : 4 * q + 4, :])
+            nc.sync.dma_start(
+                out=sc_w[32 * q + 4 : 32 * q + 8, 0 : NKV * DN].bitcast(I32), in_=ku_s[0, 4 * q : 4 * q + 4, :]
+            )
+        for s in range(1, NLOAD):
+            nc.sync.dma_start(out=x_tiles[s][:], in_=x_v[s])
+
+        kv_w = keep.tile([P, 2, DL], I32, align_bytes=64, name="kv_w")
+        trig = keep.tile([P, NT // 2, 2, 2, DR // 2], BF16, name="trig")
+
+        def permute_kv():
+            nc.vector.tensor_copy(
+                out=kv_w[:].rearrange("p g (t m) -> p g t m", t=4), in_=kv_raw[:].rearrange("p g (m t) -> p g t m", t=4)
+            )
+            nc.vector.tensor_copy(
+                out=sc_kv[:].rearrange("p (t m) -> p t m", t=4), in_=sc_raw[:].rearrange("p (m t) -> p t m", t=4)
+            )
+
+        def build_trig():
+            nc.scalar.copy(trig[:, :, 0, 0, :], cs_in[:, 0])
+            nc.scalar.copy(trig[:, :, 0, 1, :], cs_in[:, 0])
+            nc.scalar.mul(trig[:, :, 1, 0, :], cs_in[:, 1], -1.0)
+            nc.scalar.copy(trig[:, :, 1, 1, :], cs_in[:, 1])
+
+        live = [{} for n in range(NT)]
+
+        def widen(n):
+            t = live[n]
+            t["xs"] = work.tile([P, C], BF16, align_bytes=64, name="xs")
+            xb = x_tiles[n // RUN][:, n % RUN, :].bitcast(FP8)
+            if n == 0:
+                nc.vector.tensor_copy(t["xs"][:, 0:512], xb[:, 0:512])
+                nc.scalar.copy(t["xs"][:, 512:C], xb[:, 512:C])
+            else:
+                nc.gpsimd.tensor_copy(t["xs"][:], xb)
+
+        def transposes(n):
+            t = live[n]
+            words = t["xs"][:].bitcast(F32)
+            t["xt"] = ps_x.tile([P, 4, P], F32, name="xt")
+            for g in range(2):
+                for u in range(2):
+                    nc.tensor.transpose(
+                        t["xt"][:, 2 * g + u, :], words[:, 256 * g + u : 256 * (g + 1) : 2], ident[:]
+                    )
+
+        def copy_x(n):
+            t = live[n]
+            t["xg"] = work.tile([P, 2, P, 4], BF16, align_bytes=64, name="xg")
+            pairs = t["xt"][:].rearrange("p m r -> p (m r)").bitcast(BF16).rearrange("p (g u r e) -> p g u r e", g=2, u=2, e=2)
+            for g in range(2):
+                nc.vector.tensor_tensor(
+                    t["xg"][:, g].rearrange("p r (u e) -> p r u e", e=2),
+                    pairs[:, g].rearrange("p u r e -> p r u e"),
+                    xs_scale[:, g].rearrange("p (u e) -> p u e", e=2).unsqueeze(1).to_broadcast([P, P, 2, 2]),
+                    op=ALU.mult,
+                )
+
+        def quant_x(n):
+            t = live[n]
+            t["xq"] = work.tile([P, 2, P], U32, align_bytes=64, name="xq")
+            t["xqs"] = work.tile([P, 2, P], U8, align_bytes=64, name="xqs")
+            nc.vector.quantize_mx(
+                out=t["xq"][:].rearrange("p g r -> p (g r)").bitcast(FP8X4),
+                scales=t["xqs"][:].rearrange("p g r -> p (g r)"),
+                in_=t["xg"][:].rearrange("p g r j -> p (g r j)"),
+            )
+
+        def mm_lat(n):
+            t = live[n]
+            t["lat"] = ps_l.tile([P, 4, P], F32, name="lat")
+            for j in range(4):
+                for g in range(2):
+                    nc.tensor.matmul_mx(
+                        out=t["lat"][:, j, :],
+                        lhsT=kv_w[:, g, P * j : P * (j + 1)].bitcast(FP8X4),
+                        lhsT_scale=sc_kv[4 * g : P, P * j : P * (j + 1)],
+                        rhs=t["xq"][:, g, :].bitcast(FP8X4),
+                        rhs_scale=t["xqs"][:, g, :],
+                        start=(g == 0),
+                        stop=(g == 1),
+                    )
+
+        def mm_rope(n):
+            t = live[n]
+            t["kp"] = ps_k.tile([P, 2, NKV, DR], F32, name="kp")
+            for g in range(2):
+                nc.tensor.matmul_mx(
+                    out=t["kp"][:, 0].rearrange("p h d -> p (h d)"),
+                    lhsT=t["xq"][:, g, :].bitcast(FP8X4),
+                    lhsT_scale=t["xqs"][:, g, :],
+                    rhs=kr_w[:, g, :].bitcast(FP8X4),
+                    rhs_scale=sc_w[8 + 4 * g : P, 0 : NKV * DR],
+                    start=(g == 0),
+                    stop=(g == 1),
+                )
+
+        def copy_lat(n):
+            t = live[n]
+            t["lg"] = work.tile([P, P, 4], BF16, align_bytes=64, name="lg")
+            nc.scalar.copy(t["lg"][:], t["lat"][:].rearrange("p j r -> p r j"))
+
+        def quant_lat(n):
+            t = live[n]
+            t["lq"] = work.tile([P, P], U32, align_bytes=64, name="lq")
+            t["lqs"] = work.tile([P, P], U8, align_bytes=64, name="lqs")
+            nc.vector.quantize_mx(
+                out=t["lq"][:].bitcast(FP8X4), scales=t["lqs"][:], in_=t["lg"][:].rearrange("p r j -> p (r j)")
+            )
+
+        def mm_second(n):
+            t = live[n]
+            nc.tensor.matmul_mx(
+                out=t["kp"][:, 1].rearrange("p h d -> p (h d)"),
+                lhsT=t["lq"][:].bitcast(FP8X4),
+                lhsT_scale=t["lqs"][:],
+                rhs=ku_w[:].bitcast(FP8X4),
+                rhs_scale=sc_w[4:P, 0 : NKV * DN],
+                start=True,
+                stop=True,
+            )
+            t["vp"] = ps_v.tile([P, NKV * HD], F32, name="vp")
+            nc.tensor.matmul_mx(
+                out=t["vp"][:],
+                lhsT=t["lq"][:].bitcast(FP8X4),
+                lhsT_scale=t["lqs"][:],
+                rhs=vu_w[:].bitcast(FP8X4),
+                rhs_scale=sc_w[:],
+                start=True,
+                stop=True,
+            )
+
+        def rope_products(n):
+            t = live[n]
+            t["pr"] = work.tile([P, NKV, 2, 2, DR // 2], F32, name="pr")
+            shape = [P, NKV, 2, DR]
+            nc.vector.tensor_tensor(
+                t["pr"][:].rearrange("p h a b c -> p h a (b c)"),
+                t["kp"][:, 0].unsqueeze(2).to_broadcast(shape),
+                trig[:, n % (NT // 2)].rearrange("p a b c -> p a (b c)").unsqueeze(1).to_broadcast(shape),
+                op=ALU.mult,
+            )
+
+        def rope_add(n):
+            t = live[n]
+            t["kc"] = work.tile([P, NKV, HD], F32, name="kc")
+            nc.vector.tensor_tensor(
+                t["kc"][:, :, 0:DR].rearrange("p h (b c) -> p h b c", b=2),
+                t["pr"][:, :, 0],
+                t["pr"][:, :, 1, ::-1, :],
+                op=ALU.add,
+            )
+
+        def copy_nope(n):
+            t = live[n]
+            nc.scalar.copy(t["kc"][:, :, DR:HD], t["kp"][:, 1])
+
+        def copy_v(n):
+            t = live[n]
+            t["vo"] = work.tile([P, NKV * HD], F32, name="vo")
+            if n < NT - 2:
+                nc.scalar.copy(t["vo"][:], t["vp"][:])
+            else:
+                nc.vector.tensor_copy(t["vo"][:], t["vp"][:])
+            nc.sync.dma_start(out=v_v[n // RUN, n % RUN], in_=t["vo"][:])
+
+        def squares(n):
+            t = live[n]
+            t["ss"] = small.tile([P, NKV], F32, name="ss")
+            for h in range(NKV):
+                junk = work.tile([P, HD], F32, name="junk")
+                nc.scalar.activation(junk[:], t["kc"][:, h, :], ACT.Square, accum_out=t["ss"][:, h : h + 1])
+            t["sd"] = small.tile([P, NKV], F32, name="sd")
+            nc.scalar.activation(t["sd"][:], t["ss"][:], ACT.Sqrt, bias=EPS, scale=1.0 / HD)
+
+        def recip(n):
+            t = live[n]
+            t["rs"] = small.tile([P, NKV], F32, name="rs")
+            nc.vector.reciprocal(t["rs"][:], t["sd"][:])
+
+        def scale_k(n):
+            t = live[n]
+            t["ko"] = work.tile([P, NKV, HD], F32, name="ko")
+            for h in range(NKV):
+                if h < 2:
+                    nc.vector.tensor_scalar(
+                        out=t["ko"][:, h, :], in0=t["kc"][:, h, :], scalar1=t["rs"][:, h : h + 1], scalar2=None, op0=ALU.mult
+                    )
+                else:
+                    nc.scalar.activation(t["ko"][:, h, :], t["kc"][:, h, :], ACT.Copy, scale=t["rs"][:, h : h + 1])
+            nc.sync.dma_start(out=k_v[n // RUN, n % RUN], in_=t["ko"][:].rearrange("p h d -> p (h d)"))
+            live[n] = None
+
+        order = [
+            (copy_v, 4), (quant_x, 1), (rope_products, 2), (mm_second, 3), (copy_lat, 2), (mm_rope, 1), (widen, -4),
+            (copy_x, 0), (rope_add, 3), (squares, 4), (scale_k, 6), (copy_nope, 3), (recip, 5), (mm_lat, 1),
+            (transposes, -1), (quant_lat, 2),
+        ]
+        for n in range(-4, NT + 6):
+            if n == 0:
+                build_trig()
+                permute_kv()
+            for stage, lag in order:
+                if 0 <= n - lag < NT:
+                    stage(n - lag)

@@ -23,6 +23,7 @@ P = 128
 RUN = 4
 NT = TOK // P
 NLOAD = NT // RUN
+BUFS = dict(xs=6, xg=4, xq=6, lg=4, lq=4, pr=4, kc=6, ko=4, vo=4, ss=6, junk=6)
 
 
 def tile_mlacausalselfattention_pa_t_w8_kernel(
@@ -37,11 +38,13 @@ def tile_mlacausalselfattention_pa_t_w8_kernel(
     with ExitStack() as ctx:
         keep = ctx.enter_context(tc.tile_pool(name="keep", bufs=1))
         xin = ctx.enter_context(tc.tile_pool(name="xin", bufs=NLOAD))
-        work = ctx.enter_context(tc.tile_pool(name="work", bufs=4))
-        small = ctx.enter_context(tc.tile_pool(name="small", bufs=5))
-        ps_x = ctx.enter_context(tc.psum_pool(name="ps_x", bufs=1))
-        ps_l = ctx.enter_context(tc.psum_pool(name="ps_l", bufs=3))
-        ps_k = ctx.enter_context(tc.psum_pool(name="ps_k", bufs=3))
+        pools = {}
+        for name, bufs in BUFS.items():
+            pools[name] = ctx.enter_context(tc.tile_pool(name=name, bufs=bufs))
+        ps_x = ctx.enter_context(tc.psum_pool(name="ps_x", bufs=3))
+        ps_l = ctx.enter_context(tc.psum_pool(name="ps_l", bufs=2))
+        ps_r = ctx.enter_context(tc.psum_pool(name="ps_r", bufs=1))
+        ps_n = ctx.enter_context(tc.psum_pool(name="ps_n", bufs=1))
         ps_v = ctx.enter_context(tc.psum_pool(name="ps_v", bufs=1))
         ctx.enter_context(tc.manual_schedule())
 
@@ -53,7 +56,7 @@ def tile_mlacausalselfattention_pa_t_w8_kernel(
         nc.vector.memset(sc_raw[:].bitcast(I32), 0)
         nc.vector.memset(sc_w[:].bitcast(I32), 0)
         dummy_out = keep.tile([P, 1], F32, name="dummy_out")
-        nc.scalar.activation(dummy_out[:], dummy[:], ACT.Sqrt)
+        nc.scalar.activation(dummy_out[:], dummy[:], ACT.Abs_reciprocal_sqrt)
         ident = keep.tile([P, P], F32, name="ident")
         make_identity(nc, ident[:])
 
@@ -118,10 +121,13 @@ def tile_mlacausalselfattention_pa_t_w8_kernel(
 
         def widen(n):
             t = live[n]
-            t["xs"] = work.tile([P, C], BF16, align_bytes=64, name="xs")
+            t["xs"] = pools["xs"].tile([P, C], BF16, align_bytes=64, name="xs")
             xb = x_tiles[n // RUN][:, n % RUN, :].bitcast(FP8)
-            if n == 0:
+            if n < 4:
                 nc.vector.tensor_copy(t["xs"][:, 0:512], xb[:, 0:512])
+                nc.scalar.copy(t["xs"][:, 512:C], xb[:, 512:C])
+            elif n < 7:
+                nc.scalar.copy(t["xs"][:, 0:512], xb[:, 0:512])
                 nc.scalar.copy(t["xs"][:, 512:C], xb[:, 512:C])
             else:
                 nc.gpsimd.tensor_copy(t["xs"][:], xb)
@@ -138,7 +144,7 @@ def tile_mlacausalselfattention_pa_t_w8_kernel(
 
         def copy_x(n):
             t = live[n]
-            t["xg"] = work.tile([P, 2, P, 4], BF16, align_bytes=64, name="xg")
+            t["xg"] = pools["xg"].tile([P, 2, P, 4], BF16, align_bytes=64, name="xg")
             pairs = t["xt"][:].rearrange("p m r -> p (m r)").bitcast(BF16).rearrange("p (g u r e) -> p g u r e", g=2, u=2, e=2)
             for g in range(2):
                 nc.vector.tensor_tensor(
@@ -150,8 +156,8 @@ def tile_mlacausalselfattention_pa_t_w8_kernel(
 
         def quant_x(n):
             t = live[n]
-            t["xq"] = work.tile([P, 2, P], U32, align_bytes=64, name="xq")
-            t["xqs"] = work.tile([P, 2, P], U8, align_bytes=64, name="xqs")
+            t["xq"] = pools["xq"].tile([P, 2, P], U32, align_bytes=64, name="xq")
+            t["xqs"] = pools["xq"].tile([P, 2, P], U8, align_bytes=64, name="xqs")
             nc.vector.quantize_mx(
                 out=t["xq"][:].rearrange("p g r -> p (g r)").bitcast(FP8X4),
                 scales=t["xqs"][:].rearrange("p g r -> p (g r)"),
@@ -175,10 +181,10 @@ def tile_mlacausalselfattention_pa_t_w8_kernel(
 
         def mm_rope(n):
             t = live[n]
-            t["kp"] = ps_k.tile([P, 2, NKV, DR], F32, name="kp")
+            t["rp"] = ps_r.tile([P, NKV, DR], F32, name="rp")
             for g in range(2):
                 nc.tensor.matmul_mx(
-                    out=t["kp"][:, 0].rearrange("p h d -> p (h d)"),
+                    out=t["rp"][:].rearrange("p h d -> p (h d)"),
                     lhsT=t["xq"][:, g, :].bitcast(FP8X4),
                     lhsT_scale=t["xqs"][:, g, :],
                     rhs=kr_w[:, g, :].bitcast(FP8X4),
@@ -189,21 +195,25 @@ def tile_mlacausalselfattention_pa_t_w8_kernel(
 
         def copy_lat(n):
             t = live[n]
-            t["lg"] = work.tile([P, P, 4], BF16, align_bytes=64, name="lg")
-            nc.scalar.copy(t["lg"][:], t["lat"][:].rearrange("p j r -> p r j"))
+            t["lg"] = pools["lg"].tile([P, P, 4], BF16, align_bytes=64, name="lg")
+            if n < 33:
+                nc.scalar.copy(t["lg"][:], t["lat"][:].rearrange("p j r -> p r j"))
+            else:
+                nc.vector.tensor_copy(t["lg"][:], t["lat"][:].rearrange("p j r -> p r j"))
 
         def quant_lat(n):
             t = live[n]
-            t["lq"] = work.tile([P, P], U32, align_bytes=64, name="lq")
-            t["lqs"] = work.tile([P, P], U8, align_bytes=64, name="lqs")
+            t["lq"] = pools["lq"].tile([P, P], U32, align_bytes=64, name="lq")
+            t["lqs"] = pools["lq"].tile([P, P], U8, align_bytes=64, name="lqs")
             nc.vector.quantize_mx(
                 out=t["lq"][:].bitcast(FP8X4), scales=t["lqs"][:], in_=t["lg"][:].rearrange("p r j -> p (r j)")
             )
 
         def mm_second(n):
             t = live[n]
+            t["np"] = ps_n.tile([P, NKV, DN], F32, name="np")
             nc.tensor.matmul_mx(
-                out=t["kp"][:, 1].rearrange("p h d -> p (h d)"),
+                out=t["np"][:].rearrange("p h d -> p (h d)"),
                 lhsT=t["lq"][:].bitcast(FP8X4),
                 lhsT_scale=t["lqs"][:],
                 rhs=ku_w[:].bitcast(FP8X4),
@@ -224,19 +234,20 @@ def tile_mlacausalselfattention_pa_t_w8_kernel(
 
         def rope_products(n):
             t = live[n]
-            t["pr"] = work.tile([P, NKV, 2, 2, DR // 2], F32, name="pr")
+            t["pr"] = pools["pr"].tile([P, NKV, 2, 2, DR // 2], F32, name="pr")
             shape = [P, NKV, 2, DR]
             nc.vector.tensor_tensor(
                 t["pr"][:].rearrange("p h a b c -> p h a (b c)"),
-                t["kp"][:, 0].unsqueeze(2).to_broadcast(shape),
+                t["rp"][:].unsqueeze(2).to_broadcast(shape),
                 trig[:, n % (NT // 2)].rearrange("p a b c -> p a (b c)").unsqueeze(1).to_broadcast(shape),
                 op=ALU.mult,
             )
 
         def rope_add(n):
             t = live[n]
-            t["kc"] = work.tile([P, NKV, HD], F32, name="kc")
-            nc.vector.tensor_tensor(
+            t["kc"] = pools["kc"].tile([P, NKV, HD], F32, name="kc")
+            add_engine = nc.gpsimd if (n * 8) % 8 < 8 and n < 32 else nc.vector
+            add_engine.tensor_tensor(
                 t["kc"][:, :, 0:DR].rearrange("p h (b c) -> p h b c", b=2),
                 t["pr"][:, :, 0],
                 t["pr"][:, :, 1, ::-1, :],
@@ -245,12 +256,15 @@ def tile_mlacausalselfattention_pa_t_w8_kernel(
 
         def copy_nope(n):
             t = live[n]
-            nc.scalar.copy(t["kc"][:, :, DR:HD], t["kp"][:, 1])
+            if n < 31:
+                nc.scalar.copy(t["kc"][:, :, DR:HD], t["np"][:])
+            else:
+                nc.vector.tensor_copy(t["kc"][:, :, DR:HD], t["np"][:])
 
         def copy_v(n):
             t = live[n]
-            t["vo"] = work.tile([P, NKV * HD], F32, name="vo")
-            if n < NT - 2:
+            t["vo"] = pools["vo"].tile([P, NKV * HD], F32, name="vo")
+            if n < 30:
                 nc.scalar.copy(t["vo"][:], t["vp"][:])
             else:
                 nc.vector.tensor_copy(t["vo"][:], t["vp"][:])
@@ -258,23 +272,25 @@ def tile_mlacausalselfattention_pa_t_w8_kernel(
 
         def squares(n):
             t = live[n]
-            t["ss"] = small.tile([P, NKV], F32, name="ss")
+            t["ss"] = pools["ss"].tile([P, NKV], F32, name="ss")
             for h in range(NKV):
-                junk = work.tile([P, HD], F32, name="junk")
+                junk = pools["junk"].tile([P, HD], F32, name="junk")
                 nc.scalar.activation(junk[:], t["kc"][:, h, :], ACT.Square, accum_out=t["ss"][:, h : h + 1])
-            t["sd"] = small.tile([P, NKV], F32, name="sd")
-            nc.scalar.activation(t["sd"][:], t["ss"][:], ACT.Sqrt, bias=EPS, scale=1.0 / HD)
 
-        def recip(n):
+        def rsq(n):
             t = live[n]
-            t["rs"] = small.tile([P, NKV], F32, name="rs")
-            nc.vector.reciprocal(t["rs"][:], t["sd"][:])
+            t["rs"] = pools["ss"].tile([P, NKV], F32, name="rs")
+            nc.scalar.activation(t["rs"][:], t["ss"][:], ACT.Abs_reciprocal_sqrt, bias=EPS, scale=1.0 / HD)
 
         def scale_k(n):
             t = live[n]
-            t["ko"] = work.tile([P, NKV, HD], F32, name="ko")
+            t["ko"] = pools["ko"].tile([P, NKV, HD], F32, name="ko")
+            if n < 27:
+                heads_v = 2 + (1 if n % 4 < 2 else 0)
+            else:
+                heads_v = 4
             for h in range(NKV):
-                if h < 2:
+                if h < heads_v:
                     nc.vector.tensor_scalar(
                         out=t["ko"][:, h, :], in0=t["kc"][:, h, :], scalar1=t["rs"][:, h : h + 1], scalar2=None, op0=ALU.mult
                     )
@@ -284,12 +300,25 @@ def tile_mlacausalselfattention_pa_t_w8_kernel(
             live[n] = None
 
         order = [
-            (copy_v, 4), (quant_x, 1), (rope_products, 2), (mm_second, 3), (copy_lat, 2), (mm_rope, 1), (widen, -4),
-            (copy_x, 0), (rope_add, 3), (squares, 4), (scale_k, 6), (copy_nope, 3), (recip, 5), (mm_lat, 1),
-            (transposes, -1), (quant_lat, 2),
+            (rope_products, 6),
+            (mm_rope, 5),
+            (copy_lat, 6),
+            (scale_k, 9),
+            (rsq, 8),
+            (rope_add, 6),
+            (widen, 0),
+            (copy_nope, 7),
+            (copy_v, 7),
+            (quant_lat, 6),
+            (mm_second, 6),
+            (quant_x, 4),
+            (mm_lat, 4),
+            (squares, 7),
+            (copy_x, 3),
+            (transposes, 1),
         ]
-        for n in range(-4, NT + 6):
-            if n == 0:
+        for n in range(0, NT + 9):
+            if n == 3:
                 build_trig()
                 permute_kv()
             for stage, lag in order:

@@ -41,11 +41,11 @@ def tile_mlacausalselfattention_pa_t_w8_kernel(
         pools = {}
         for name, bufs in BUFS.items():
             pools[name] = ctx.enter_context(tc.tile_pool(name=name, bufs=bufs))
-        ps_x = ctx.enter_context(tc.psum_pool(name="ps_x", bufs=3))
+        ps_x = ctx.enter_context(tc.psum_pool(name="ps_x", bufs=2))
         ps_l = ctx.enter_context(tc.psum_pool(name="ps_l", bufs=2))
         ps_r = ctx.enter_context(tc.psum_pool(name="ps_r", bufs=1))
         ps_n = ctx.enter_context(tc.psum_pool(name="ps_n", bufs=1))
-        ps_v = ctx.enter_context(tc.psum_pool(name="ps_v", bufs=1))
+        ps_v = ctx.enter_context(tc.psum_pool(name="ps_v", bufs=2))
         ctx.enter_context(tc.manual_schedule())
 
         sc_raw = keep.tile([P, DL], U8, align_bytes=64, name="sc_raw")
@@ -73,6 +73,7 @@ def tile_mlacausalselfattention_pa_t_w8_kernel(
         kv_s = w_kv_scales.bitcast(I32)
         for q in range(4):
             nc.sync.dma_start(out=sc_raw[32 * q : 32 * q + 8, :].bitcast(I32), in_=kv_s[:, 4 * q : 4 * q + 4, :])
+        nc.sync.dma_start(out=x_tiles[1][:], in_=x_v[1])
         kr_w = keep.tile([P, 2, NKV * DR], I32, align_bytes=64, name="kr_w")
         nc.sync.dma_start(out=kr_w[:], in_=w_krope_words.rearrange("g p n t -> p g (n t)").bitcast(I32))
         kr_s = w_krope_scales.bitcast(I32)
@@ -97,17 +98,17 @@ def tile_mlacausalselfattention_pa_t_w8_kernel(
             nc.sync.dma_start(
                 out=sc_w[32 * q + 4 : 32 * q + 8, 0 : NKV * DN].bitcast(I32), in_=ku_s[0, 4 * q : 4 * q + 4, :]
             )
-        for s in range(1, NLOAD):
+        for s in range(2, NLOAD):
             nc.sync.dma_start(out=x_tiles[s][:], in_=x_v[s])
 
         kv_w = keep.tile([P, 2, DL], I32, align_bytes=64, name="kv_w")
         trig = keep.tile([P, NT // 2, 2, 2, DR // 2], BF16, name="trig")
 
         def permute_kv():
-            nc.vector.tensor_copy(
+            nc.gpsimd.tensor_copy(
                 out=kv_w[:].rearrange("p g (t m) -> p g t m", t=4), in_=kv_raw[:].rearrange("p g (m t) -> p g t m", t=4)
             )
-            nc.vector.tensor_copy(
+            nc.gpsimd.tensor_copy(
                 out=sc_kv[:].rearrange("p (t m) -> p t m", t=4), in_=sc_raw[:].rearrange("p (m t) -> p t m", t=4)
             )
 
@@ -123,10 +124,10 @@ def tile_mlacausalselfattention_pa_t_w8_kernel(
             t = live[n]
             t["xs"] = pools["xs"].tile([P, C], BF16, align_bytes=64, name="xs")
             xb = x_tiles[n // RUN][:, n % RUN, :].bitcast(FP8)
-            if n < 4:
+            if n < 2:
                 nc.vector.tensor_copy(t["xs"][:, 0:512], xb[:, 0:512])
                 nc.scalar.copy(t["xs"][:, 512:C], xb[:, 512:C])
-            elif n < 7:
+            elif n < 5:
                 nc.scalar.copy(t["xs"][:, 0:512], xb[:, 0:512])
                 nc.scalar.copy(t["xs"][:, 512:C], xb[:, 512:C])
             else:
@@ -196,7 +197,7 @@ def tile_mlacausalselfattention_pa_t_w8_kernel(
         def copy_lat(n):
             t = live[n]
             t["lg"] = pools["lg"].tile([P, P, 4], BF16, align_bytes=64, name="lg")
-            if n < 33:
+            if n < 30:
                 nc.scalar.copy(t["lg"][:], t["lat"][:].rearrange("p j r -> p r j"))
             else:
                 nc.vector.tensor_copy(t["lg"][:], t["lat"][:].rearrange("p j r -> p r j"))
@@ -256,7 +257,7 @@ def tile_mlacausalselfattention_pa_t_w8_kernel(
 
         def copy_nope(n):
             t = live[n]
-            if n < 31:
+            if n < 33:
                 nc.scalar.copy(t["kc"][:, :, DR:HD], t["np"][:])
             else:
                 nc.vector.tensor_copy(t["kc"][:, :, DR:HD], t["np"][:])
@@ -285,8 +286,8 @@ def tile_mlacausalselfattention_pa_t_w8_kernel(
         def scale_k(n):
             t = live[n]
             t["ko"] = pools["ko"].tile([P, NKV, HD], F32, name="ko")
-            if n < 27:
-                heads_v = 2 + (1 if n % 4 < 2 else 0)
+            if n < 21:
+                heads_v = 1 + (1 if n % 4 < 1 else 0)
             else:
                 heads_v = 4
             for h in range(NKV):
@@ -300,27 +301,28 @@ def tile_mlacausalselfattention_pa_t_w8_kernel(
             live[n] = None
 
         order = [
-            (rope_products, 6),
-            (mm_rope, 5),
-            (copy_lat, 6),
-            (scale_k, 9),
-            (rsq, 8),
-            (rope_add, 6),
-            (widen, 0),
-            (copy_nope, 7),
-            (copy_v, 7),
-            (quant_lat, 6),
-            (mm_second, 6),
-            (quant_x, 4),
-            (mm_lat, 4),
-            (squares, 7),
-            (copy_x, 3),
-            (transposes, 1),
+            (scale_k, 12),
+            (copy_v, 10),
+            (copy_lat, 8),
+            (mm_rope, 8),
+            (squares, 10),
+            (mm_second, 9),
+            (copy_x, 4),
+            (rope_products, 8),
+            (mm_lat, 7),
+            (transposes, 3),
+            (widen, 2),
+            (copy_nope, 9),
+            (quant_lat, 8),
+            (quant_x, 6),
+            (rope_add, 8),
+            (rsq, 10),
         ]
-        for n in range(0, NT + 9):
-            if n == 3:
-                build_trig()
+        for n in range(2, NT + 12):
+            if n == 7:
                 permute_kv()
+            if n == 8:
+                build_trig()
             for stage, lag in order:
                 if 0 <= n - lag < NT:
                     stage(n - lag)

from contextlib import ExitStack

import concourse.mybir as mybir
from concourse.masks import make_identity

B, T, C, DL = 2, 2048, 1024, 512
NKV, HD, DR, DN = 4, 128, 64, 64
TOK = B * T
EPS = 1.1920928955078125e-07
FLOPS = 2 * TOK * (C * DL + DL * NKV * DN + DL * NKV * HD + C * NKV * DR)

F32 = mybir.dt.float32
BF16 = mybir.dt.bfloat16
I32 = mybir.dt.int32
U32 = mybir.dt.uint32
U8 = mybir.dt.uint8
FP8 = mybir.dt.float8_e4m3fn
FP8X4 = mybir.dt.float8_e4m3fn_x4
ACT = mybir.ActivationFunctionType
ALU = mybir.AluOpType

P = 128
RUN = 4
NT = TOK // P
NLOAD = NT // RUN
BUFS = dict(xs=6, xg=4, xq=6, lg=4, lq=4, pr=4, kc=6, ko=4, vo=4, ss=6, junk=6)


def tile_mlacausalselfattention_pa_t_w8_kernel(
    tc, x_bytes, x_scale, cos, sin, w_kv_words, w_kv_scales, w_kup_words, w_kup_scales,
    w_vup_words, w_vup_scales, w_krope_words, w_krope_scales, out_k, out_v,
):
    nc = tc.nc
    x_v = x_bytes.rearrange("b t k -> (b t) k").rearrange("(s p i) k -> s p i k", p=P, i=RUN)
    k_v = out_k.rearrange("b t h d -> (b t) (h d)").rearrange("(s p i) c -> s i p c", p=P, i=RUN)
    v_v = out_v.rearrange("b t h d -> (b t) (h d)").rearrange("(s p i) c -> s i p c", p=P, i=RUN)

    with ExitStack() as ctx:
        keep = ctx.enter_context(tc.tile_pool(name="keep", bufs=1))
        xin = ctx.enter_context(tc.tile_pool(name="xin", bufs=NLOAD))
        pools = {}
        for name, bufs in BUFS.items():
            pools[name] = ctx.enter_context(tc.tile_pool(name=name, bufs=bufs))
        ps_x = ctx.enter_context(tc.psum_pool(name="ps_x", bufs=2))
        ps_l = ctx.enter_context(tc.psum_pool(name="ps_l", bufs=2))
        ps_r = ctx.enter_context(tc.psum_pool(name="ps_r", bufs=1))
        ps_n = ctx.enter_context(tc.psum_pool(name="ps_n", bufs=1))
        ps_v = ctx.enter_context(tc.psum_pool(name="ps_v", bufs=2))
        ctx.enter_context(tc.manual_schedule())

        sc_raw = keep.tile([P, DL], U8, align_bytes=64, name="sc_raw")
        sc_w = keep.tile([P, DL], U8, align_bytes=64, name="sc_w")
        sc_kv = keep.tile([P, DL], U8, align_bytes=64, name="sc_kv")
        dummy = keep.tile([P, 1], F32, name="dummy")
        nc.vector.memset(dummy[:], 1.0)
        nc.vector.memset(sc_raw[:].bitcast(I32), 0)
        nc.vector.memset(sc_w[:].bitcast(I32), 0)
        dummy_out = keep.tile([P, 1], F32, name="dummy_out")
        nc.scalar.activation(dummy_out[:], dummy[:], ACT.Abs_reciprocal_sqrt)
        ident = keep.tile([P, P], F32, name="ident")
        make_identity(nc, ident[:])

        xs_scale = keep.tile([P, 2, 4], F32, name="xs_scale")
        x_tiles = []
        for s in range(NLOAD):
            xt_in = xin.tile([P, RUN, C], U8, align_bytes=64, name="xt_in")
            x_tiles.append(xt_in)
        nc.sync.dma_start(out=x_tiles[0][:, 0, :], in_=x_v[0][:, 0, :])
        nc.sync.dma_start(out=xs_scale[:], in_=x_scale.rearrange("a b (g p t) -> p (a b g) t", p=P, t=4))
        nc.sync.dma_start(out=x_tiles[0][:, 1:RUN, :], in_=x_v[0][:, 1:RUN, :])
        kv_raw = keep.tile([P, 2, DL], I32, align_bytes=64, name="kv_raw")
        nc.sync.dma_start(out=kv_raw[:], in_=w_kv_words.rearrange("g p n t -> p g (n t)").bitcast(I32))
        kv_s = w_kv_scales.bitcast(I32)
        for q in range(4):
            nc.sync.dma_start(out=sc_raw[32 * q : 32 * q + 8, :].bitcast(I32), in_=kv_s[:, 4 * q : 4 * q + 4, :])
        nc.sync.dma_start(out=x_tiles[1][:], in_=x_v[1])
        kr_w = keep.tile([P, 2, NKV * DR], I32, align_bytes=64, name="kr_w")
        nc.sync.dma_start(out=kr_w[:], in_=w_krope_words.rearrange("g p n t -> p g (n t)").bitcast(I32))
        kr_s = w_krope_scales.bitcast(I32)
        for q in range(4):
            nc.sync.dma_start(
                out=sc_w[32 * q + 8 : 32 * q + 16, 0 : NKV * DR].bitcast(I32), in_=kr_s[:, 4 * q : 4 * q + 4, :]
            )
        cs_in = keep.tile([P, 2, NT // 2, DR // 2], BF16, name="cs_in")
        for j, src in enumerate((cos, sin)):
            nc.sync.dma_start(
                out=cs_in[:, j].rearrange("p (s i) c -> p s i c", i=RUN),
                in_=src.rearrange("(s p i) c -> p s i c", p=P, i=RUN),
            )
        ku_w = keep.tile([P, NKV * DN], I32, align_bytes=64, name="ku_w")
        nc.sync.dma_start(out=ku_w[:], in_=w_kup_words[0].rearrange("p n t -> p (n t)").bitcast(I32))
        vu_w = keep.tile([P, NKV * HD], I32, align_bytes=64, name="vu_w")
        nc.sync.dma_start(out=vu_w[:], in_=w_vup_words[0].rearrange("p n t -> p (n t)").bitcast(I32))
        vu_s = w_vup_scales.bitcast(I32)
        ku_s = w_kup_scales.bitcast(I32)
        for q in range(4):
            nc.sync.dma_start(out=sc_w[32 * q : 32 * q + 4, :].bitcast(I32), in_=vu_s[0, 4 * q : 4 * q + 4, :])
            nc.sync.dma_start(
                out=sc_w[32 * q + 4 : 32 * q + 8, 0 : NKV * DN].bitcast(I32), in_=ku_s[0, 4 * q : 4 * q + 4, :]
            )
        for s in range(2, NLOAD):
            nc.sync.dma_start(out=x_tiles[s][:], in_=x_v[s])

        kv_w = keep.tile([P, 2, DL], I32, align_bytes=64, name="kv_w")
        trig = keep.tile([P, NT // 2, 2, 2, DR // 2], BF16, name="trig")

        def permute_kv():
            nc.gpsimd.tensor_copy(
                out=kv_w[:].rearrange("p g (t m) -> p g t m", t=4), in_=kv_raw[:].rearrange("p g (m t) -> p g t m", t=4)
            )
            nc.gpsimd.tensor_copy(
                out=sc_kv[:].rearrange("p (t m) -> p t m", t=4), in_=sc_raw[:].rearrange("p (m t) -> p t m", t=4)
            )

        def build_trig():
            nc.scalar.copy(trig[:, :, 0, 0, :], cs_in[:, 0])
            nc.scalar.copy(trig[:, :, 0, 1, :], cs_in[:, 0])
            nc.scalar.mul(trig[:, :, 1, 0, :], cs_in[:, 1], -1.0)
            nc.scalar.copy(trig[:, :, 1, 1, :], cs_in[:, 1])

        live = [{} for n in range(NT)]

        def widen(n):
            t = live[n]
            t["xs"] = pools["xs"].tile([P, C], BF16, align_bytes=64, name="xs")
            xb = x_tiles[n // RUN][:, n % RUN, :].bitcast(FP8)
            if n < 2:
                nc.vector.tensor_copy(t["xs"][:, 0:512], xb[:, 0:512])
                nc.scalar.copy(t["xs"][:, 512:C], xb[:, 512:C])
            elif n < 5:
                nc.scalar.copy(t["xs"][:, 0:512], xb[:, 0:512])
                nc.scalar.copy(t["xs"][:, 512:C], xb[:, 512:C])
            else:
                nc.gpsimd.tensor_copy(t["xs"][:], xb)

        def transposes(n):
            t = live[n]
            words = t["xs"][:].bitcast(F32)
            t["xt"] = ps_x.tile([P, 4, P], F32, name="xt")
            for g in range(2):
                for u in range(2):
                    nc.tensor.transpose(
                        t["xt"][:, 2 * g + u, :], words[:, 256 * g + u : 256 * (g + 1) : 2], ident[:]
                    )

        def copy_x(n):
            t = live[n]
            t["xg"] = pools["xg"].tile([P, 2, P, 4], BF16, align_bytes=64, name="xg")
            pairs = t["xt"][:].rearrange("p m r -> p (m r)").bitcast(BF16).rearrange("p (g u r e) -> p g u r e", g=2, u=2, e=2)
            for g in range(2):
                nc.vector.tensor_tensor(
                    t["xg"][:, g].rearrange("p r (u e) -> p r u e", e=2),
                    pairs[:, g].rearrange("p u r e -> p r u e"),
                    xs_scale[:, g].rearrange("p (u e) -> p u e", e=2).unsqueeze(1).to_broadcast([P, P, 2, 2]),
                    op=ALU.mult,
                )

        def quant_x(n):
            t = live[n]
            t["xq"] = pools["xq"].tile([P, 2, P], U32, align_bytes=64, name="xq")
            t["xqs"] = pools["xq"].tile([P, 2, P], U8, align_bytes=64, name="xqs")
            nc.vector.quantize_mx(
                out=t["xq"][:].rearrange("p g r -> p (g r)").bitcast(FP8X4),
                scales=t["xqs"][:].rearrange("p g r -> p (g r)"),
                in_=t["xg"][:].rearrange("p g r j -> p (g r j)"),
            )

        def mm_lat(n):
            t = live[n]
            t["lat"] = ps_l.tile([P, 4, P], F32, name="lat")
            for j in range(4):
                for g in range(2):
                    nc.tensor.matmul_mx(
                        out=t["lat"][:, j, :],
                        lhsT=kv_w[:, g, P * j : P * (j + 1)].bitcast(FP8X4),
                        lhsT_scale=sc_kv[4 * g : P, P * j : P * (j + 1)],
                        rhs=t["xq"][:, g, :].bitcast(FP8X4),
                        rhs_scale=t["xqs"][:, g, :],
                        start=(g == 0),
                        stop=(g == 1),
                    )

        def mm_rope(n):
            t = live[n]
            t["rp"] = ps_r.tile([P, NKV, DR], F32, name="rp")
            for g in range(2):
                nc.tensor.matmul_mx(
                    out=t["rp"][:].rearrange("p h d -> p (h d)"),
                    lhsT=t["xq"][:, g, :].bitcast(FP8X4),
                    lhsT_scale=t["xqs"][:, g, :],
                    rhs=kr_w[:, g, :].bitcast(FP8X4),
                    rhs_scale=sc_w[8 + 4 * g : P, 0 : NKV * DR],
                    start=(g == 0),
                    stop=(g == 1),
                )

        def copy_lat(n):
            t = live[n]
            t["lg"] = pools["lg"].tile([P, P, 4], BF16, align_bytes=64, name="lg")
            if n < 30:
                nc.scalar.copy(t["lg"][:], t["lat"][:].rearrange("p j r -> p r j"))
            else:
                nc.vector.tensor_copy(t["lg"][:], t["lat"][:].rearrange("p j r -> p r j"))

        def quant_lat(n):
            t = live[n]
            t["lq"] = pools["lq"].tile([P, P], U32, align_bytes=64, name="lq")
            t["lqs"] = pools["lq"].tile([P, P], U8, align_bytes=64, name="lqs")
            nc.vector.quantize_mx(
                out=t["lq"][:].bitcast(FP8X4), scales=t["lqs"][:], in_=t["lg"][:].rearrange("p r j -> p (r j)")
            )

        def mm_second(n):
            t = live[n]
            t["np"] = ps_n.tile([P, NKV, DN], F32, name="np")
            nc.tensor.matmul_mx(
                out=t["np"][:].rearrange("p h d -> p (h d)"),
                lhsT=t["lq"][:].bitcast(FP8X4),
                lhsT_scale=t["lqs"][:],
                rhs=ku_w[:].bitcast(FP8X4),
                rhs_scale=sc_w[4:P, 0 : NKV * DN],
                start=True,
                stop=True,
            )
            t["vp"] = ps_v.tile([P, NKV * HD], F32, name="vp")
            nc.tensor.matmul_mx(
                out=t["vp"][:],
                lhsT=t["lq"][:].bitcast(FP8X4),
                lhsT_scale=t["lqs"][:],
                rhs=vu_w[:].bitcast(FP8X4),
                rhs_scale=sc_w[:],
                start=True,
                stop=True,
            )

        def rope_products(n):
            t = live[n]
            t["pr"] = pools["pr"].tile([P, NKV, 2, 2, DR // 2], F32, name="pr")
            shape = [P, NKV, 2, DR]
            nc.vector.tensor_tensor(
                t["pr"][:].rearrange("p h a b c -> p h a (b c)"),
                t["rp"][:].unsqueeze(2).to_broadcast(shape),
                trig[:, n % (NT // 2)].rearrange("p a b c -> p a (b c)").unsqueeze(1).to_broadcast(shape),
                op=ALU.mult,
            )

        def rope_add(n):
            t = live[n]
            t["kc"] = pools["kc"].tile([P, NKV, HD], F32, name="kc")
            add_engine = nc.gpsimd if (n * 8) % 8 < 8 and n < 32 else nc.vector
            add_engine.tensor_tensor(
                t["kc"][:, :, 0:DR].rearrange("p h (b c) -> p h b c", b=2),
                t["pr"][:, :, 0],
                t["pr"][:, :, 1, ::-1, :],
                op=ALU.add,
            )

        def copy_nope(n):
            t = live[n]
            if n < 33:
                nc.scalar.copy(t["kc"][:, :, DR:HD], t["np"][:])
            else:
                nc.vector.tensor_copy(t["kc"][:, :, DR:HD], t["np"][:])

        def copy_v(n):
            t = live[n]
            t["vo"] = pools["vo"].tile([P, NKV * HD], F32, name="vo")
            if n < 30:
                nc.scalar.copy(t["vo"][:], t["vp"][:])
            else:
                nc.vector.tensor_copy(t["vo"][:], t["vp"][:])
            nc.sync.dma_start(out=v_v[n // RUN, n % RUN], in_=t["vo"][:])

        def squares(n):
            t = live[n]
            t["ss"] = pools["ss"].tile([P, NKV], F32, name="ss")
            for h in range(NKV):
                junk = pools["junk"].tile([P, HD], F32, name="junk")
                nc.scalar.activation(junk[:], t["kc"][:, h, :], ACT.Square, accum_out=t["ss"][:, h : h + 1])

        def rsq(n):
            t = live[n]
            t["rs"] = pools["ss"].tile([P, NKV], F32, name="rs")
            nc.scalar.activation(t["rs"][:], t["ss"][:], ACT.Abs_reciprocal_sqrt, bias=EPS, scale=1.0 / HD)

        def scale_k(n):
            t = live[n]
            t["ko"] = pools["ko"].tile([P, NKV, HD], F32, name="ko")
            if n < 21:
                heads_v = 1 + (1 if n % 4 < 1 else 0)
            else:
                heads_v = 4
            for h in range(NKV):
                if h < heads_v:
                    nc.vector.tensor_scalar(
                        out=t["ko"][:, h, :], in0=t["kc"][:, h, :], scalar1=t["rs"][:, h : h + 1], scalar2=None, op0=ALU.mult
                    )
                else:
                    nc.scalar.activation(t["ko"][:, h, :], t["kc"][:, h, :], ACT.Copy, scale=t["rs"][:, h : h + 1])
            nc.sync.dma_start(out=k_v[n // RUN, n % RUN], in_=t["ko"][:].rearrange("p h d -> p (h d)"))
            live[n] = None

        order = [
            (scale_k, 12),
            (copy_v, 10),
            (copy_lat, 8),
            (mm_rope, 8),
            (squares, 10),
            (mm_second, 9),
            (copy_x, 4),
            (rope_products, 8),
            (mm_lat, 7),
            (transposes, 3),
            (widen, 2),
            (copy_nope, 9),
            (quant_lat, 8),
            (quant_x, 6),
            (rope_add, 8),
            (rsq, 10),
        ]
        for n in range(2, NT + 12):
            if n == 7:
                permute_kv()
            if n == 8:
                build_trig()
            for stage, lag in order:
                if 0 <= n - lag < NT:
                    stage(n - lag)
